import numpy as np
import ml_dtypes


def mxq(x, axis, fmt="e4m3"):
    dtype, down = {"e4m3": (ml_dtypes.float8_e4m3fn, 7), "e5m2": (ml_dtypes.float8_e5m2, 14)}[fmt]
    v = np.moveaxis(np.asarray(x, np.float32).astype(ml_dtypes.bfloat16).astype(np.float64), axis, -1)
    blocks = v.reshape(v.shape[:-1] + (-1, 32))
    amax = np.abs(blocks).max(-1, keepdims=True)
    byte = np.maximum(np.where(amax > 0, np.frexp(amax)[1] - 1 + 127, 0) - down, 1)
    scale = np.exp2(byte - 127.0)
    codes = (blocks / scale).astype(np.float32).astype(dtype).astype(np.float64)
    return np.moveaxis((codes * scale).reshape(v.shape), -1, axis)


WIDE = False


def mx_kscale(k):
    if not WIDE:
        return np.ones(k)
    levels = np.array([10, -10, 5, -5, 0])
    a = np.random.permutation(np.resize(levels, k // 512 * 4)).reshape(k // 512, 4)
    idx = np.arange(k)
    return np.exp2(a[idx // 512, idx % 128 // 32])


BF16 = ml_dtypes.bfloat16


def bf(x):
    return np.asarray(x, np.float32).astype(BF16)


def f64(x):
    return np.asarray(x).astype(np.float64)


B, S, K, H, D = 16, 384, 128, 512, 256
EPS = 1e-6


def setup_inputs():
    s = mx_kscale(H)
    rows = 0.5 * np.exp(0.5 * np.random.standard_normal((B, S, 1)))
    return {"hidden_states": bf(np.random.standard_normal((B, S, H)) * rows),
            "memory_state": bf(np.random.standard_normal((B, K, H)) * s),
            "q_w": bf(np.random.standard_normal((D, H)) * 1.5 / np.sqrt(H) / s),
            "k_w": bf(np.random.standard_normal((D, H)) * 1.5 / np.sqrt(H) / s),
            "norm_w": bf((1.0 + 0.3 * np.random.standard_normal(H)) * s)}


def reference(hidden_states, memory_state, q_w, k_w, norm_w):
    x = f64(hidden_states)
    normed = x * (1.0 / np.sqrt(np.mean(x * x, axis=-1, keepdims=True) + EPS)) * f64(norm_w)
    pool = np.concatenate([normed, f64(memory_state)], axis=1)
    pq = mxq(pool, 2, "e4m3")
    q = pq[:, :S] @ mxq(f64(q_w), 1, "e4m3").T
    k = pq @ mxq(f64(k_w), 1, "e4m3").T
    return q, k

@@ -1,0 +1,188 @@
+from contextlib import ExitStack
+
+import concourse.mybir as mybir
+from concourse.masks import make_identity
+
+F32 = mybir.dt.float32
+BF16 = mybir.dt.bfloat16
+U32 = mybir.dt.uint32
+U8 = mybir.dt.uint8
+FP8X4 = mybir.dt.float8_e4m3fn_x4
+ACT = mybir.ActivationFunctionType
+ALU = mybir.AluOpType
+
+P = 128
+PACK = 4
+B = 16
+S = 384
+H = 512
+D = 256
+EPS = 1e-6
+TOKEN_TILES = S // P
+POOL_TILES = TOKEN_TILES + 1
+MEMORY_LOAD = 4
+
+FLOPS = 2 * B * (S + S + P) * D * H
+
+
+def tile_memresprojections_pa_t_kernel(
+    tc, hidden_states, memory_state, q_w, k_w, norm_w, out_0, out_1
+):
+    nc = tc.nc
+    with ExitStack() as ctx:
+        keep = ctx.enter_context(tc.tile_pool(name="keep", bufs=1))
+        stats = ctx.enter_context(tc.tile_pool(name="stats", bufs=4))
+        squares = ctx.enter_context(tc.tile_pool(name="squares", bufs=4))
+        scaled_pool = ctx.enter_context(tc.tile_pool(name="scaled", bufs=6))
+        grouped_pool = ctx.enter_context(tc.tile_pool(name="grouped", bufs=3))
+        mx_pool = ctx.enter_context(tc.tile_pool(name="mx", bufs=3))
+        result_pool = ctx.enter_context(tc.tile_pool(name="result", bufs=5))
+        turned_psum = ctx.enter_context(tc.psum_pool(name="turned", bufs=4))
+        acc_psum = ctx.enter_context(tc.psum_pool(name="acc", bufs=4))
+
+        eps = keep.tile([P, 1], F32)
+        nc.vector.memset(eps[:], EPS)
+        warm = keep.tile([P, 1], F32)
+        nc.scalar.activation(out=warm[:], in_=eps[:], func=ACT.Sqrt)
+        ident = keep.tile([P, P], F32)
+        make_identity(nc, ident[:])
+
+        x_all = keep.tile([P, B, TOKEN_TILES, H], BF16)
+        mem_all = keep.tile([P, B, H], BF16)
+        w_raw = keep.tile([P, 2, 2, H], BF16)
+        gain = keep.tile([P, 2, 2], BF16)
+
+        def load_hidden(b):
+            nc.sync.dma_start(
+                out=x_all[:, b], in_=hidden_states[b].rearrange("(p j) h -> p j h", j=TOKEN_TILES)
+            )
+
+        load_hidden(0)
+        nc.sync.dma_start(out=gain[:], in_=norm_w.rearrange("(u p e) -> p u e", u=2, e=2))
+        nc.sync.dma_start(out=w_raw[:, 0], in_=q_w.rearrange("(r p) h -> p r h", p=P))
+        nc.sync.dma_start(out=w_raw[:, 1], in_=k_w.rearrange("(r p) h -> p r h", p=P))
+        for b in range(B):
+            if b % MEMORY_LOAD == 0:
+                nc.sync.dma_start(
+                    out=mem_all[:, b : b + MEMORY_LOAD],
+                    in_=memory_state[b : b + MEMORY_LOAD].rearrange("b p h -> p b h"),
+                )
+            if b + 1 < B:
+                load_hidden(b + 1)
+
+        w_grouped = keep.tile([P, 2 * D, PACK], BF16, align_bytes=64)
+        w_codes = keep.tile([P, 2 * D], U32, align_bytes=64)
+        w_scales = keep.tile([P, 2 * D], U8, align_bytes=64)
+        w_words = w_grouped[:].rearrange("p c t -> p (c t)").bitcast(F32)
+        for m in range(2):
+            w_turned = turned_psum.tile([P, 2, D], F32, tag="turned")
+            for r in range(2):
+                for u in range(2):
+                    nc.tensor.transpose(
+                        w_turned[:, u, r * P : (r + 1) * P],
+                        w_raw[:, m, r, :].bitcast(F32)[:, u * P : (u + 1) * P],
+                        ident[:],
+                    )
+            nc.vector.tensor_copy(
+                out=w_words[:, m * 2 * D : (m + 1) * 2 * D].rearrange("p (c u) -> p c u", u=2),
+                in_=w_turned[:].rearrange("p u c -> p c u"),
+            )
+        nc.vector.quantize_mx(
+            out=w_codes[:].bitcast(FP8X4),
+            scales=w_scales[:],
+            in_=w_grouped[:].rearrange("p c t -> p (c t)"),
+        )
+
+        for b in range(B):
+            sumsq = stats.tile([P, TOKEN_TILES], F32)
+            for j in range(TOKEN_TILES):
+                unused = squares.tile([P, H], BF16)
+                nc.scalar.activation(
+                    out=unused[:], in_=x_all[:, b, j, :], func=ACT.Square,
+                    accum_out=sumsq[:, j : j + 1],
+                )
+            rms = stats.tile([P, TOKEN_TILES], F32)
+            nc.scalar.activation(out=rms[:], in_=sumsq[:], func=ACT.Sqrt, bias=eps[:, 0:1], scale=1.0 / H)
+            rstd = stats.tile([P, TOKEN_TILES], F32)
+            nc.vector.reciprocal(out=rstd[:], in_=rms[:])
+
+            grouped = grouped_pool.tile([P, POOL_TILES, P, PACK], BF16, align_bytes=64)
+            for j in range(TOKEN_TILES):
+                scaled = scaled_pool.tile([P, PACK, P], F32)
+                nc.gpsimd.tensor_scalar(
+                    out=scaled[:].rearrange("p (u e) i -> p u e i", e=2),
+                    in0=x_all[:, b, j, :].rearrange("p (u i e) -> p u e i", u=2, e=2),
+                    scalar1=rstd[:, j : j + 1],
+                    scalar2=1.0,
+                    op0=ALU.mult,
+                    op1=ALU.mult,
+                )
+                turned = turned_psum.tile([P, PACK, P], F32, tag="turned")
+                for t in range(PACK):
+                    nc.tensor.transpose(turned[:, t, :], scaled[:, t, :], ident[:])
+                nc.vector.tensor_tensor(
+                    out=grouped[:, j],
+                    in0=turned[:].rearrange("p t k -> p k t"),
+                    in1=gain[:].rearrange("p u e -> p (u e)").unsqueeze(1).to_broadcast([P, P, PACK]),
+                    op=ALU.mult,
+                )
+            mem_turned = turned_psum.tile([P, 2, P], F32, tag="turned")
+            for u in range(2):
+                nc.tensor.transpose(
+                    mem_turned[:, u, :],
+                    mem_all[:, b, :].bitcast(F32)[:, u * P : (u + 1) * P],
+                    ident[:],
+                )
+            nc.vector.tensor_copy(
+                out=grouped[:, TOKEN_TILES].rearrange("p k t -> p (k t)").bitcast(F32)
+                .rearrange("p (k u) -> p k u", u=2),
+                in_=mem_turned[:].rearrange("p u k -> p k u"),
+            )
+
+            codes = mx_pool.tile([P, POOL_TILES * P], U32, align_bytes=64)
+            scales = mx_pool.tile([P, POOL_TILES * P], U8, align_bytes=64)
+            nc.vector.quantize_mx(
+                out=codes[:].bitcast(FP8X4),
+                scales=scales[:],
+                in_=grouped[:].rearrange("p j k t -> p (j k t)"),
+            )
+
+            qk = result_pool.tile([P, 2, TOKEN_TILES, D], F32)
+            for j in range(TOKEN_TILES):
+                cols = slice(j * P, (j + 1) * P)
+                acc = acc_psum.tile([P, 2 * D], F32, tag="acc")
+                nc.tensor.matmul_mx(
+                    out=acc[:],
+                    lhsT=codes[:, cols].bitcast(FP8X4),
+                    lhsT_scale=scales[:, cols],
+                    rhs=w_codes[:].bitcast(FP8X4),
+                    rhs_scale=w_scales[:],
+                    start=True,
+                    stop=True,
+                )
+                source = acc[:].rearrange("p (m d) -> p m d", m=2)
+                if j == TOKEN_TILES - 1:
+                    nc.vector.tensor_copy(out=qk[:, :, j, :], in_=source)
+                else:
+                    nc.scalar.copy(out=qk[:, :, j, :], in_=source)
+            cols = slice(TOKEN_TILES * P, POOL_TILES * P)
+            mem_acc = acc_psum.tile([P, D], F32, tag="acc")
+            nc.tensor.matmul_mx(
+                out=mem_acc[:],
+                lhsT=codes[:, cols].bitcast(FP8X4),
+                lhsT_scale=scales[:, cols],
+                rhs=w_codes[:, D : 2 * D].bitcast(FP8X4),
+                rhs_scale=w_scales[:, D : 2 * D],
+                start=True,
+                stop=True,
+            )
+            k_mem = result_pool.tile([P, D], F32)
+            nc.scalar.copy(out=k_mem[:], in_=mem_acc[:])
+
+            nc.sync.dma_start(
+                out=out_0[b].rearrange("(p j) d -> p j d", j=TOKEN_TILES), in_=qk[:, 0]
+            )
+            nc.sync.dma_start(
+                out=out_1[b, 0:S, :].rearrange("(p j) d -> p j d", j=TOKEN_TILES), in_=qk[:, 1]
+            )
+            nc.sync.dma_start(out=out_1[b, S : S + P, :], in_=k_mem[:])

@@ -24,6 +24,10 @@ MEMORY_LOAD = 4
 
 FLOPS = 2 * B * (S + S + P) * D * H
 
+SQUARES_AHEAD = 3
+SCALE_AHEAD = 2
+TURN_AHEAD = 1
+
 
 def tile_memresprojections_pa_t_kernel(
     tc, hidden_states, memory_state, q_w, k_w, norm_w, out_0, out_1
@@ -32,13 +36,14 @@ def tile_memresprojections_pa_t_kernel(
     with ExitStack() as ctx:
         keep = ctx.enter_context(tc.tile_pool(name="keep", bufs=1))
         stats = ctx.enter_context(tc.tile_pool(name="stats", bufs=4))
-        squares = ctx.enter_context(tc.tile_pool(name="squares", bufs=4))
-        scaled_pool = ctx.enter_context(tc.tile_pool(name="scaled", bufs=6))
-        grouped_pool = ctx.enter_context(tc.tile_pool(name="grouped", bufs=3))
+        squares_pool = ctx.enter_context(tc.tile_pool(name="squares", bufs=4))
+        scaled_pool = ctx.enter_context(tc.tile_pool(name="scaled", bufs=2 * TOKEN_TILES))
+        grouped_pool = ctx.enter_context(tc.tile_pool(name="grouped", bufs=2))
         mx_pool = ctx.enter_context(tc.tile_pool(name="mx", bufs=3))
         result_pool = ctx.enter_context(tc.tile_pool(name="result", bufs=5))
-        turned_psum = ctx.enter_context(tc.psum_pool(name="turned", bufs=4))
-        acc_psum = ctx.enter_context(tc.psum_pool(name="acc", bufs=4))
+        turned_psum = ctx.enter_context(tc.psum_pool(name="turned", bufs=POOL_TILES))
+        acc_psum = ctx.enter_context(tc.psum_pool(name="acc", bufs=POOL_TILES))
+        ctx.enter_context(tc.manual_schedule())
 
         eps = keep.tile([P, 1], F32)
         nc.vector.memset(eps[:], EPS)
@@ -61,124 +66,126 @@ def tile_memresprojections_pa_t_kernel(
         nc.sync.dma_start(out=gain[:], in_=norm_w.rearrange("(u p e) -> p u e", u=2, e=2))
         nc.sync.dma_start(out=w_raw[:, 0], in_=q_w.rearrange("(r p) h -> p r h", p=P))
         nc.sync.dma_start(out=w_raw[:, 1], in_=k_w.rearrange("(r p) h -> p r h", p=P))
-        for b in range(B):
-            if b % MEMORY_LOAD == 0:
+        for b in range(1, B):
+            load_hidden(b)
+            if b % MEMORY_LOAD == 1:
+                first = b - 1
                 nc.sync.dma_start(
-                    out=mem_all[:, b : b + MEMORY_LOAD],
-                    in_=memory_state[b : b + MEMORY_LOAD].rearrange("b p h -> p b h"),
+                    out=mem_all[:, first : first + MEMORY_LOAD],
+                    in_=memory_state[first : first + MEMORY_LOAD].rearrange("b p h -> p b h"),
                 )
-            if b + 1 < B:
-                load_hidden(b + 1)
 
-        w_grouped = keep.tile([P, 2 * D, PACK], BF16, align_bytes=64)
-        w_codes = keep.tile([P, 2 * D], U32, align_bytes=64)
-        w_scales = keep.tile([P, 2 * D], U8, align_bytes=64)
-        w_words = w_grouped[:].rearrange("p c t -> p (c t)").bitcast(F32)
-        for m in range(2):
-            w_turned = turned_psum.tile([P, 2, D], F32, tag="turned")
-            for r in range(2):
-                for u in range(2):
-                    nc.tensor.transpose(
-                        w_turned[:, u, r * P : (r + 1) * P],
-                        w_raw[:, m, r, :].bitcast(F32)[:, u * P : (u + 1) * P],
-                        ident[:],
-                    )
-            nc.vector.tensor_copy(
-                out=w_words[:, m * 2 * D : (m + 1) * 2 * D].rearrange("p (c u) -> p c u", u=2),
-                in_=w_turned[:].rearrange("p u c -> p c u"),
-            )
-        nc.vector.quantize_mx(
-            out=w_codes[:].bitcast(FP8X4),
-            scales=w_scales[:],
-            in_=w_grouped[:].rearrange("p c t -> p (c t)"),
-        )
+        rms_of = {}
+        rstd_of = {}
+        scaled_of = {}
+        turned_of = {}
+        grouped_of = {}
+        codes_of = {}
+        scales_of = {}
+        acc_of = {}
+        result_of = {}
 
-        for b in range(B):
+        def squares(b):
             sumsq = stats.tile([P, TOKEN_TILES], F32)
             for j in range(TOKEN_TILES):
-                unused = squares.tile([P, H], BF16)
+                unused = squares_pool.tile([P, H], BF16)
                 nc.scalar.activation(
                     out=unused[:], in_=x_all[:, b, j, :], func=ACT.Square,
                     accum_out=sumsq[:, j : j + 1],
                 )
-            rms = stats.tile([P, TOKEN_TILES], F32)
-            nc.scalar.activation(out=rms[:], in_=sumsq[:], func=ACT.Sqrt, bias=eps[:, 0:1], scale=1.0 / H)
-            rstd = stats.tile([P, TOKEN_TILES], F32)
-            nc.vector.reciprocal(out=rstd[:], in_=rms[:])
+            rms_of[b] = stats.tile([P, TOKEN_TILES], F32, name="rms")
+            nc.scalar.activation(
+                out=rms_of[b][:], in_=sumsq[:], func=ACT.Sqrt, bias=eps[:, 0:1], scale=1.0 / H
+            )
 
-            grouped = grouped_pool.tile([P, POOL_TILES, P, PACK], BF16, align_bytes=64)
+        def reciprocal(b):
+            rstd_of[b] = stats.tile([P, TOKEN_TILES], F32, name="rstd")
+            nc.vector.reciprocal(out=rstd_of[b][:], in_=rms_of[b][:])
+
+        def scale(b):
             for j in range(TOKEN_TILES):
-                scaled = scaled_pool.tile([P, PACK, P], F32)
+                scaled = scaled_pool.tile([P, PACK, P], F32, name="scaled")
+                scaled_of[b, j] = scaled
                 nc.gpsimd.tensor_scalar(
                     out=scaled[:].rearrange("p (u e) i -> p u e i", e=2),
                     in0=x_all[:, b, j, :].rearrange("p (u i e) -> p u e i", u=2, e=2),
-                    scalar1=rstd[:, j : j + 1],
+                    scalar1=rstd_of[b][:, j : j + 1],
                     scalar2=1.0,
                     op0=ALU.mult,
                     op1=ALU.mult,
                 )
-                turned = turned_psum.tile([P, PACK, P], F32, tag="turned")
+
+        def turn(b):
+            for j in range(TOKEN_TILES):
+                turned = turned_psum.tile([P, PACK, P], F32, name="turned")
+                turned_of[b, j] = turned
                 for t in range(PACK):
-                    nc.tensor.transpose(turned[:, t, :], scaled[:, t, :], ident[:])
+                    nc.tensor.transpose(turned[:, t, :], scaled_of[b, j][:, t, :], ident[:])
+            turned = turned_psum.tile([P, 2, P], F32, name="turned")
+            turned_of[b, TOKEN_TILES] = turned
+            for u in range(2):
+                nc.tensor.transpose(
+                    turned[:, u, :], mem_all[:, b, :].bitcast(F32)[:, u * P : (u + 1) * P], ident[:]
+                )
+
+        def leave(b, scalar_is_free):
+            grouped = grouped_pool.tile([P, POOL_TILES, P, PACK], BF16, align_bytes=64, name="grouped")
+            grouped_of[b] = grouped
+            for j in range(TOKEN_TILES):
                 nc.vector.tensor_tensor(
                     out=grouped[:, j],
-                    in0=turned[:].rearrange("p t k -> p k t"),
+                    in0=turned_of[b, j][:].rearrange("p t k -> p k t"),
                     in1=gain[:].rearrange("p u e -> p (u e)").unsqueeze(1).to_broadcast([P, P, PACK]),
                     op=ALU.mult,
                 )
-            mem_turned = turned_psum.tile([P, 2, P], F32, tag="turned")
-            for u in range(2):
-                nc.tensor.transpose(
-                    mem_turned[:, u, :],
-                    mem_all[:, b, :].bitcast(F32)[:, u * P : (u + 1) * P],
-                    ident[:],
-                )
-            nc.vector.tensor_copy(
-                out=grouped[:, TOKEN_TILES].rearrange("p k t -> p (k t)").bitcast(F32)
-                .rearrange("p (k u) -> p k u", u=2),
-                in_=mem_turned[:].rearrange("p u k -> p k u"),
+            words = (
+                grouped[:, TOKEN_TILES].rearrange("p k t -> p (k t)").bitcast(F32)
+                .rearrange("p (k u) -> p k u", u=2)
             )
+            source = turned_of[b, TOKEN_TILES][:].rearrange("p u k -> p k u")
+            if scalar_is_free:
+                nc.scalar.copy(out=words, in_=source)
+            else:
+                nc.vector.tensor_copy(out=words, in_=source)
 
-            codes = mx_pool.tile([P, POOL_TILES * P], U32, align_bytes=64)
-            scales = mx_pool.tile([P, POOL_TILES * P], U8, align_bytes=64)
+        def quantise(b):
+            codes_of[b] = mx_pool.tile([P, POOL_TILES * P], U32, align_bytes=64, name="codes")
+            scales_of[b] = mx_pool.tile([P, POOL_TILES * P], U8, align_bytes=64, name="scales")
             nc.vector.quantize_mx(
-                out=codes[:].bitcast(FP8X4),
-                scales=scales[:],
-                in_=grouped[:].rearrange("p j k t -> p (j k t)"),
+                out=codes_of[b][:].bitcast(FP8X4),
+                scales=scales_of[b][:],
+                in_=grouped_of[b][:].rearrange("p j k t -> p (j k t)"),
             )
 
-            qk = result_pool.tile([P, 2, TOKEN_TILES, D], F32)
-            for j in range(TOKEN_TILES):
+        def multiply(b):
+            for j in range(POOL_TILES):
+                first = 0 if j < TOKEN_TILES else D
                 cols = slice(j * P, (j + 1) * P)
-                acc = acc_psum.tile([P, 2 * D], F32, tag="acc")
+                acc_of[b, j] = acc_psum.tile([P, 2 * D - first], F32, name="acc")
                 nc.tensor.matmul_mx(
-                    out=acc[:],
-                    lhsT=codes[:, cols].bitcast(FP8X4),
-                    lhsT_scale=scales[:, cols],
-                    rhs=w_codes[:].bitcast(FP8X4),
-                    rhs_scale=w_scales[:],
+                    out=acc_of[b, j][:],
+                    lhsT=codes_of[b][:, cols].bitcast(FP8X4),
+                    lhsT_scale=scales_of[b][:, cols],
+                    rhs=w_codes[:, first : 2 * D].bitcast(FP8X4),
+                    rhs_scale=w_scales[:, first : 2 * D],
                     start=True,
                     stop=True,
                 )
-                source = acc[:].rearrange("p (m d) -> p m d", m=2)
-                if j == TOKEN_TILES - 1:
-                    nc.vector.tensor_copy(out=qk[:, :, j, :], in_=source)
-                else:
-                    nc.scalar.copy(out=qk[:, :, j, :], in_=source)
-            cols = slice(TOKEN_TILES * P, POOL_TILES * P)
-            mem_acc = acc_psum.tile([P, D], F32, tag="acc")
-            nc.tensor.matmul_mx(
-                out=mem_acc[:],
-                lhsT=codes[:, cols].bitcast(FP8X4),
-                lhsT_scale=scales[:, cols],
-                rhs=w_codes[:, D : 2 * D].bitcast(FP8X4),
-                rhs_scale=w_scales[:, D : 2 * D],
-                start=True,
-                stop=True,
-            )
-            k_mem = result_pool.tile([P, D], F32)
-            nc.scalar.copy(out=k_mem[:], in_=mem_acc[:])
 
+        def copy_out(b, scalar_is_free):
+            qk = result_pool.tile([P, 2, TOKEN_TILES, D], F32, name="qk")
+            k_mem = result_pool.tile([P, D], F32, name="k_mem")
+            result_of[b] = (qk, k_mem)
+            for j in range(TOKEN_TILES):
+                source = acc_of[b, j][:].rearrange("p (m d) -> p m d", m=2)
+                if j < TOKEN_TILES - 1 or scalar_is_free:
+                    nc.scalar.copy(out=qk[:, :, j, :], in_=source)
+                else:
+                    nc.vector.tensor_copy(out=qk[:, :, j, :], in_=source)
+            nc.scalar.copy(out=k_mem[:], in_=acc_of[b, TOKEN_TILES][:])
+
+        def store(b):
+            qk, k_mem = result_of[b]
             nc.sync.dma_start(
                 out=out_0[b].rearrange("(p j) d -> p j d", j=TOKEN_TILES), in_=qk[:, 0]
             )
@@ -186,3 +193,50 @@ def tile_memresprojections_pa_t_kernel(
                 out=out_1[b, 0:S, :].rearrange("(p j) d -> p j d", j=TOKEN_TILES), in_=qk[:, 1]
             )
             nc.sync.dma_start(out=out_1[b, S : S + P, :], in_=k_mem[:])
+
+        w_grouped = keep.tile([P, 2 * D, PACK], BF16, align_bytes=64)
+        w_codes = keep.tile([P, 2 * D], U32, align_bytes=64)
+        w_scales = keep.tile([P, 2 * D], U8, align_bytes=64)
+
+        def prepare_weights():
+            w_words = w_grouped[:].rearrange("p c t -> p (c t)").bitcast(F32)
+            for m in range(2):
+                w_turned = turned_psum.tile([P, 2, D], F32, name="turned")
+                for r in range(2):
+                    for u in range(2):
+                        nc.tensor.transpose(
+                            w_turned[:, u, r * P : (r + 1) * P],
+                            w_raw[:, m, r, :].bitcast(F32)[:, u * P : (u + 1) * P],
+                            ident[:],
+                        )
+                nc.vector.tensor_copy(
+                    out=w_words[:, m * 2 * D : (m + 1) * 2 * D].rearrange("p (c u) -> p c u", u=2),
+                    in_=w_turned[:].rearrange("p u c -> p c u"),
+                )
+            nc.vector.quantize_mx(
+                out=w_codes[:].bitcast(FP8X4),
+                scales=w_scales[:],
+                in_=w_grouped[:].rearrange("p c t -> p (c t)"),
+            )
+
+        squares(0)
+        reciprocal(0)
+        prepare_weights()
+        for step in range(1 - SQUARES_AHEAD, B):
+            scalar_is_free = step + SQUARES_AHEAD >= B
+            if step + SQUARES_AHEAD < B:
+                squares(step + SQUARES_AHEAD)
+            if 0 <= step + SCALE_AHEAD < B:
+                scale(step + SCALE_AHEAD)
+            if 0 <= step + TURN_AHEAD < B:
+                turn(step + TURN_AHEAD)
+                leave(step + TURN_AHEAD, scalar_is_free)
+            if step >= 0:
+                multiply(step)
+                copy_out(step, scalar_is_free)
+            if 0 <= step + TURN_AHEAD < B:
+                quantise(step + TURN_AHEAD)
+            if step + SQUARES_AHEAD < B:
+                reciprocal(step + SQUARES_AHEAD)
+            if step >= 0:
+                store(step)

@@ -172,17 +172,20 @@ def tile_memresprojections_pa_t_kernel(
                     stop=True,
                 )
 
-        def copy_out(b, scalar_is_free):
+        def copy_out(b, vector_helps):
             qk = result_pool.tile([P, 2, TOKEN_TILES, D], F32, name="qk")
             k_mem = result_pool.tile([P, D], F32, name="k_mem")
             result_of[b] = (qk, k_mem)
             for j in range(TOKEN_TILES):
                 source = acc_of[b, j][:].rearrange("p (m d) -> p m d", m=2)
-                if j < TOKEN_TILES - 1 or scalar_is_free:
-                    nc.scalar.copy(out=qk[:, :, j, :], in_=source)
-                else:
+                if j == TOKEN_TILES - 1 and vector_helps:
                     nc.vector.tensor_copy(out=qk[:, :, j, :], in_=source)
-            nc.scalar.copy(out=k_mem[:], in_=acc_of[b, TOKEN_TILES][:])
+                else:
+                    nc.scalar.copy(out=qk[:, :, j, :], in_=source)
+            if vector_helps:
+                nc.vector.tensor_copy(out=k_mem[:], in_=acc_of[b, TOKEN_TILES][:])
+            else:
+                nc.scalar.copy(out=k_mem[:], in_=acc_of[b, TOKEN_TILES][:])
 
         def store(b):
             qk, k_mem = result_of[b]
@@ -224,6 +227,7 @@ def tile_memresprojections_pa_t_kernel(
         prepare_weights()
         for step in range(1 - SQUARES_AHEAD, B):
             scalar_is_free = step + SQUARES_AHEAD >= B
+            vector_helps = not scalar_is_free or step + TURN_AHEAD >= B
             if step + SQUARES_AHEAD < B:
                 squares(step + SQUARES_AHEAD)
             if 0 <= step + SCALE_AHEAD < B:
@@ -233,7 +237,7 @@ def tile_memresprojections_pa_t_kernel(
                 leave(step + TURN_AHEAD, scalar_is_free)
             if step >= 0:
                 multiply(step)
-                copy_out(step, scalar_is_free)
+                copy_out(step, vector_helps)
             if 0 <= step + TURN_AHEAD < B:
                 quantise(step + TURN_AHEAD)
             if step + SQUARES_AHEAD < B:

@@ -106,7 +106,7 @@ def tile_memresprojections_pa_t_kernel(
             for j in range(TOKEN_TILES):
                 scaled = scaled_pool.tile([P, PACK, P], F32, name="scaled")
                 scaled_of[b, j] = scaled
-                nc.gpsimd.tensor_scalar(
+                nc.vector.tensor_scalar(
                     out=scaled[:].rearrange("p (u e) i -> p u e i", e=2),
                     in0=x_all[:, b, j, :].rearrange("p (u i e) -> p u e i", u=2, e=2),
                     scalar1=rstd_of[b][:, j : j + 1],
@@ -172,20 +172,17 @@ def tile_memresprojections_pa_t_kernel(
                     stop=True,
                 )
 
-        def copy_out(b, vector_helps):
+        def copy_out(b, scalar_is_free):
             qk = result_pool.tile([P, 2, TOKEN_TILES, D], F32, name="qk")
             k_mem = result_pool.tile([P, D], F32, name="k_mem")
             result_of[b] = (qk, k_mem)
             for j in range(TOKEN_TILES):
                 source = acc_of[b, j][:].rearrange("p (m d) -> p m d", m=2)
-                if j == TOKEN_TILES - 1 and vector_helps:
-                    nc.vector.tensor_copy(out=qk[:, :, j, :], in_=source)
-                else:
+                if j < TOKEN_TILES - 1 or scalar_is_free:
                     nc.scalar.copy(out=qk[:, :, j, :], in_=source)
-            if vector_helps:
-                nc.vector.tensor_copy(out=k_mem[:], in_=acc_of[b, TOKEN_TILES][:])
-            else:
-                nc.scalar.copy(out=k_mem[:], in_=acc_of[b, TOKEN_TILES][:])
+                else:
+                    nc.vector.tensor_copy(out=qk[:, :, j, :], in_=source)
+            nc.scalar.copy(out=k_mem[:], in_=acc_of[b, TOKEN_TILES][:])
 
         def store(b):
             qk, k_mem = result_of[b]
@@ -227,7 +224,6 @@ def tile_memresprojections_pa_t_kernel(
         prepare_weights()
         for step in range(1 - SQUARES_AHEAD, B):
             scalar_is_free = step + SQUARES_AHEAD >= B
-            vector_helps = not scalar_is_free or step + TURN_AHEAD >= B
             if step + SQUARES_AHEAD < B:
                 squares(step + SQUARES_AHEAD)
             if 0 <= step + SCALE_AHEAD < B:
@@ -237,7 +233,7 @@ def tile_memresprojections_pa_t_kernel(
                 leave(step + TURN_AHEAD, scalar_is_free)
             if step >= 0:
                 multiply(step)
-                copy_out(step, vector_helps)
+                copy_out(step, True)
             if 0 <= step + TURN_AHEAD < B:
                 quantise(step + TURN_AHEAD)
             if step + SQUARES_AHEAD < B:

from contextlib import ExitStack

import concourse.mybir as mybir
from concourse.masks import make_identity

F32 = mybir.dt.float32
BF16 = mybir.dt.bfloat16
U32 = mybir.dt.uint32
U8 = mybir.dt.uint8
FP8X4 = mybir.dt.float8_e4m3fn_x4
ACT = mybir.ActivationFunctionType
ALU = mybir.AluOpType

P = 128
PACK = 4
B = 16
S = 384
H = 512
D = 256
EPS = 1e-6
TOKEN_TILES = S // P
POOL_TILES = TOKEN_TILES + 1
MEMORY_LOAD = 4

FLOPS = 2 * B * (S + S + P) * D * H

SQUARES_AHEAD = 3
SCALE_AHEAD = 2
TURN_AHEAD = 1


def tile_memresprojections_pa_t_kernel(
    tc, hidden_states, memory_state, q_w, k_w, norm_w, out_0, out_1
):
    nc = tc.nc
    with ExitStack() as ctx:
        keep = ctx.enter_context(tc.tile_pool(name="keep", bufs=1))
        stats = ctx.enter_context(tc.tile_pool(name="stats", bufs=4))
        squares_pool = ctx.enter_context(tc.tile_pool(name="squares", bufs=4))
        scaled_pool = ctx.enter_context(tc.tile_pool(name="scaled", bufs=2 * TOKEN_TILES))
        grouped_pool = ctx.enter_context(tc.tile_pool(name="grouped", bufs=2))
        mx_pool = ctx.enter_context(tc.tile_pool(name="mx", bufs=3))
        result_pool = ctx.enter_context(tc.tile_pool(name="result", bufs=5))
        turned_psum = ctx.enter_context(tc.psum_pool(name="turned", bufs=POOL_TILES))
        acc_psum = ctx.enter_context(tc.psum_pool(name="acc", bufs=POOL_TILES))
        ctx.enter_context(tc.manual_schedule())

        eps = keep.tile([P, 1], F32)
        nc.vector.memset(eps[:], EPS)
        warm = keep.tile([P, 1], F32)
        nc.scalar.activation(out=warm[:], in_=eps[:], func=ACT.Sqrt)
        ident = keep.tile([P, P], F32)
        make_identity(nc, ident[:])

        x_all = keep.tile([P, B, TOKEN_TILES, H], BF16)
        mem_all = keep.tile([P, B, H], BF16)
        w_raw = keep.tile([P, 2, 2, H], BF16)
        gain = keep.tile([P, 2, 2], BF16)

        def load_hidden(b):
            nc.sync.dma_start(
                out=x_all[:, b], in_=hidden_states[b].rearrange("(p j) h -> p j h", j=TOKEN_TILES)
            )

        load_hidden(0)
        nc.sync.dma_start(out=gain[:], in_=norm_w.rearrange("(u p e) -> p u e", u=2, e=2))
        nc.sync.dma_start(out=w_raw[:, 0], in_=q_w.rearrange("(r p) h -> p r h", p=P))
        nc.sync.dma_start(out=w_raw[:, 1], in_=k_w.rearrange("(r p) h -> p r h", p=P))
        for b in range(1, B):
            load_hidden(b)
            if b % MEMORY_LOAD == 1:
                first = b - 1
                nc.sync.dma_start(
                    out=mem_all[:, first : first + MEMORY_LOAD],
                    in_=memory_state[first : first + MEMORY_LOAD].rearrange("b p h -> p b h"),
                )

        rms_of = {}
        rstd_of = {}
        scaled_of = {}
        turned_of = {}
        grouped_of = {}
        codes_of = {}
        scales_of = {}
        acc_of = {}
        result_of = {}

        def squares(b):
            sumsq = stats.tile([P, TOKEN_TILES], F32)
            for j in range(TOKEN_TILES):
                unused = squares_pool.tile([P, H], BF16)
                nc.scalar.activation(
                    out=unused[:], in_=x_all[:, b, j, :], func=ACT.Square,
                    accum_out=sumsq[:, j : j + 1],
                )
            rms_of[b] = stats.tile([P, TOKEN_TILES], F32, name="rms")
            nc.scalar.activation(
                out=rms_of[b][:], in_=sumsq[:], func=ACT.Sqrt, bias=eps[:, 0:1], scale=1.0 / H
            )

        def reciprocal(b):
            rstd_of[b] = stats.tile([P, TOKEN_TILES], F32, name="rstd")
            nc.vector.reciprocal(out=rstd_of[b][:], in_=rms_of[b][:])

        def scale(b):
            for j in range(TOKEN_TILES):
                scaled = scaled_pool.tile([P, PACK, P], F32, name="scaled")
                scaled_of[b, j] = scaled
                nc.vector.tensor_scalar(
                    out=scaled[:].rearrange("p (u e) i -> p u e i", e=2),
                    in0=x_all[:, b, j, :].rearrange("p (u i e) -> p u e i", u=2, e=2),
                    scalar1=rstd_of[b][:, j : j + 1],
                    scalar2=1.0,
                    op0=ALU.mult,
                    op1=ALU.mult,
                )

        def turn(b):
            for j in range(TOKEN_TILES):
                turned = turned_psum.tile([P, PACK, P], F32, name="turned")
                turned_of[b, j] = turned
                for t in range(PACK):
                    nc.tensor.transpose(turned[:, t, :], scaled_of[b, j][:, t, :], ident[:])
            turned = turned_psum.tile([P, 2, P], F32, name="turned")
            turned_of[b, TOKEN_TILES] = turned
            for u in range(2):
                nc.tensor.transpose(
                    turned[:, u, :], mem_all[:, b, :].bitcast(F32)[:, u * P : (u + 1) * P], ident[:]
                )

        def leave(b, scalar_is_free):
            grouped = grouped_pool.tile([P, POOL_TILES, P, PACK], BF16, align_bytes=64, name="grouped")
            grouped_of[b] = grouped
            for j in range(TOKEN_TILES):
                nc.vector.tensor_tensor(
                    out=grouped[:, j],
                    in0=turned_of[b, j][:].rearrange("p t k -> p k t"),
                    in1=gain[:].rearrange("p u e -> p (u e)").unsqueeze(1).to_broadcast([P, P, PACK]),
                    op=ALU.mult,
                )
            words = (
                grouped[:, TOKEN_TILES].rearrange("p k t -> p (k t)").bitcast(F32)
                .rearrange("p (k u) -> p k u", u=2)
            )
            source = turned_of[b, TOKEN_TILES][:].rearrange("p u k -> p k u")
            if scalar_is_free:
                nc.scalar.copy(out=words, in_=source)
            else:
                nc.vector.tensor_copy(out=words, in_=source)

        def quantise(b):
            codes_of[b] = mx_pool.tile([P, POOL_TILES * P], U32, align_bytes=64, name="codes")
            scales_of[b] = mx_pool.tile([P, POOL_TILES * P], U8, align_bytes=64, name="scales")
            nc.vector.quantize_mx(
                out=codes_of[b][:].bitcast(FP8X4),
                scales=scales_of[b][:],
                in_=grouped_of[b][:].rearrange("p j k t -> p (j k t)"),
            )

        def multiply(b):
            for j in range(POOL_TILES):
                first = 0 if j < TOKEN_TILES else D
                cols = slice(j * P, (j + 1) * P)
                acc_of[b, j] = acc_psum.tile([P, 2 * D - first], F32, name="acc")
                nc.tensor.matmul_mx(
                    out=acc_of[b, j][:],
                    lhsT=codes_of[b][:, cols].bitcast(FP8X4),
                    lhsT_scale=scales_of[b][:, cols],
                    rhs=w_codes[:, first : 2 * D].bitcast(FP8X4),
                    rhs_scale=w_scales[:, first : 2 * D],
                    start=True,
                    stop=True,
                )

        def copy_out(b, scalar_is_free):
            qk = result_pool.tile([P, 2, TOKEN_TILES, D], F32, name="qk")
            k_mem = result_pool.tile([P, D], F32, name="k_mem")
            result_of[b] = (qk, k_mem)
            for j in range(TOKEN_TILES):
                source = acc_of[b, j][:].rearrange("p (m d) -> p m d", m=2)
                if j < TOKEN_TILES - 1 or scalar_is_free:
                    nc.scalar.copy(out=qk[:, :, j, :], in_=source)
                else:
                    nc.vector.tensor_copy(out=qk[:, :, j, :], in_=source)
            nc.scalar.copy(out=k_mem[:], in_=acc_of[b, TOKEN_TILES][:])

        def store(b):
            qk, k_mem = result_of[b]
            nc.sync.dma_start(
                out=out_0[b].rearrange("(p j) d -> p j d", j=TOKEN_TILES), in_=qk[:, 0]
            )
            nc.sync.dma_start(
                out=out_1[b, 0:S, :].rearrange("(p j) d -> p j d", j=TOKEN_TILES), in_=qk[:, 1]
            )
            nc.sync.dma_start(out=out_1[b, S : S + P, :], in_=k_mem[:])

        w_grouped = keep.tile([P, 2 * D, PACK], BF16, align_bytes=64)
        w_codes = keep.tile([P, 2 * D], U32, align_bytes=64)
        w_scales = keep.tile([P, 2 * D], U8, align_bytes=64)

        def prepare_weights():
            w_words = w_grouped[:].rearrange("p c t -> p (c t)").bitcast(F32)
            for m in range(2):
                w_turned = turned_psum.tile([P, 2, D], F32, name="turned")
                for r in range(2):
                    for u in range(2):
                        nc.tensor.transpose(
                            w_turned[:, u, r * P : (r + 1) * P],
                            w_raw[:, m, r, :].bitcast(F32)[:, u * P : (u + 1) * P],
                            ident[:],
                        )
                nc.vector.tensor_copy(
                    out=w_words[:, m * 2 * D : (m + 1) * 2 * D].rearrange("p (c u) -> p c u", u=2),
                    in_=w_turned[:].rearrange("p u c -> p c u"),
                )
            nc.vector.quantize_mx(
                out=w_codes[:].bitcast(FP8X4),
                scales=w_scales[:],
                in_=w_grouped[:].rearrange("p c t -> p (c t)"),
            )

        squares(0)
        reciprocal(0)
        prepare_weights()
        for step in range(1 - SQUARES_AHEAD, B):
            scalar_is_free = step + SQUARES_AHEAD >= B
            if step + SQUARES_AHEAD < B:
                squares(step + SQUARES_AHEAD)
            if 0 <= step + SCALE_AHEAD < B:
                scale(step + SCALE_AHEAD)
            if 0 <= step + TURN_AHEAD < B:
                turn(step + TURN_AHEAD)
                leave(step + TURN_AHEAD, scalar_is_free)
            if step >= 0:
                multiply(step)
                copy_out(step, True)
            if 0 <= step + TURN_AHEAD < B:
                quantise(step + TURN_AHEAD)
            if step + SQUARES_AHEAD < B:
                reciprocal(step + SQUARES_AHEAD)
            if step >= 0:
                store(step)
